import numpy as np
import ml_dtypes


def mxq(x, axis, fmt="e4m3"):
    dtype, down = {"e4m3": (ml_dtypes.float8_e4m3fn, 7), "e5m2": (ml_dtypes.float8_e5m2, 14)}[fmt]
    v = np.moveaxis(np.asarray(x, np.float32).astype(ml_dtypes.bfloat16).astype(np.float64), axis, -1)
    blocks = v.reshape(v.shape[:-1] + (-1, 32))
    amax = np.abs(blocks).max(-1, keepdims=True)
    byte = np.maximum(np.where(amax > 0, np.frexp(amax)[1] - 1 + 127, 0) - down, 1)
    scale = np.exp2(byte - 127.0)
    codes = (blocks / scale).astype(np.float32).astype(dtype).astype(np.float64)
    return np.moveaxis((codes * scale).reshape(v.shape), -1, axis)


WIDE = False


def mx_kscale(k):
    if not WIDE:
        return np.ones(k)
    levels = np.array([10, -10, 5, -5, 0])
    a = np.random.permutation(np.resize(levels, k // 512 * 4)).reshape(k // 512, 4)
    idx = np.arange(k)
    return np.exp2(a[idx // 512, idx % 128 // 32])


BF16 = ml_dtypes.bfloat16


def bf(x):
    return np.asarray(x, np.float32).astype(BF16)


def f64(x):
    return np.asarray(x).astype(np.float64)


E2M1 = np.array([0.0, 0.5, 1.0, 1.5, 2.0, 3.0, 4.0, 6.0, -0.0, -0.5, -1.0, -1.5, -2.0, -3.0, -4.0, -6.0])


def pack_weight(w, fmt):
    k, n = w.shape
    w = f64(bf(w)).reshape(k // 32, 32, n)
    amax = np.abs(w).max(1)
    if fmt == "e4m3":
        byte = np.frexp(amax)[1] - 1 + 127 - 7
    else:
        mant, ex = np.frexp(amax / 6.0)
        byte = np.where(mant > 0.5, ex, ex - 1) + 127
    byte = np.clip(np.where(amax > 0, byte, 1), 1, 254)
    scaled = (w * np.exp2(127.0 - byte)[:, None, :]).reshape(k, n).astype(np.float32)
    by_word = np.ascontiguousarray(scaled.reshape(k // 512, 128, 4, n).transpose(0, 1, 3, 2))
    if fmt == "e4m3":
        words = by_word.astype(ml_dtypes.float8_e4m3fn).view(np.uint8)
    else:
        c = by_word.astype(ml_dtypes.float4_e2m1fn).view(np.uint8) & 0xF
        words = c[..., 0::2] | (c[..., 1::2] << 4)
    return np.ascontiguousarray(words), np.ascontiguousarray(byte.astype(np.uint8).reshape(k // 512, 16, n))


def unpack_weight(words, scales, fmt):
    g, p, n, _ = words.shape
    if fmt == "e4m3":
        vals = np.ascontiguousarray(words).view(ml_dtypes.float8_e4m3fn).astype(np.float64)
    else:
        nib = np.empty((g, p, n, 4), np.uint8)
        nib[..., 0::2] = words & 0xF
        nib[..., 1::2] = words >> 4
        vals = E2M1[nib]
    vals = vals * np.repeat(np.exp2(scales.astype(np.float64) - 127.0), 8, axis=1)[..., None]
    return vals.transpose(0, 1, 3, 2).reshape(g * 512, n)

def pack4(w):
    words, scales = pack_weight(w, "e2m1")
    return words.reshape(words.shape[0], 128, -1), scales


def unpack4(words, scales):
    return unpack_weight(words.reshape(words.shape[0], 128, -1, 2), scales, "e2m1")


B, N, K, H, C_E, M = 2, 8, 16, 1024, 1024, 16384
SCALE = 30.0


def setup_inputs():
    s = mx_kscale(M)
    h2 = bf(np.random.standard_normal((B, N, K, M)) * 0.65 * s)
    h_V = bf(np.random.standard_normal((B, N, H)))
    mask_attend = bf(np.random.uniform(size=(B, N, K)) < 0.9)
    words, scales = pack4(np.random.standard_normal((M, H)) * 4.0 / np.sqrt(M) / s[:, None])
    W3_b = bf(np.random.standard_normal(H) * 0.1)
    return {"h2": h2,
            "h_V": h_V,
            "mask_attend": mask_attend,
            "W3_w_words": words,
            "W3_w_scales": scales,
            "W3_b": W3_b}


def reference(h2, h_V, mask_attend, W3_w_words, W3_w_scales, W3_b):
    h_message = (mxq(f64(h2), 3, "e4m3") @ unpack4(W3_w_words, W3_w_scales)) + f64(W3_b)
    h_message = f64(mask_attend)[..., None] * h_message
    dh = np.sum(h_message, axis=-2) / SCALE
    return f64(h_V) + dh

@@ -1,0 +1,241 @@
+from contextlib import ExitStack
+
+import concourse.mybir as mybir
+from concourse.masks import make_identity
+
+F32 = mybir.dt.float32
+BF16 = mybir.dt.bfloat16
+I32 = mybir.dt.int32
+U32 = mybir.dt.uint32
+U8 = mybir.dt.uint8
+FP8X4 = mybir.dt.float8_e4m3fn_x4
+FP4X4 = mybir.dt.float4_e2m1fn_x4
+ADD = mybir.AluOpType.add
+MULT = mybir.AluOpType.mult
+
+P = 128
+PACK = 4
+K_PASS = P * PACK
+PAIR = 2
+
+NODES = 16
+EDGES = 16
+K = 16384
+H = 1024
+DIVISOR = 30.0
+
+ROW_TILES = NODES * EDGES // P
+K_STEPS = K // K_PASS
+PSUM_BANKS = 8
+N_TILE = 512
+N_TILES = H // N_TILE
+SCALE_ROWS = K_PASS // 32
+
+ROUND = 4
+ROUNDS = K_STEPS // ROUND
+BANK_STEPS = 2
+AHEAD = 4
+
+FLOPS = 2 * NODES * EDGES * K * H
+
+
+def tile_declayerj_pb_k_kernel(tc, h2, h_V, mask_attend, W3_w_words, W3_w_scales, W3_b, out):
+    nc = tc.nc
+    h2_rows = h2.rearrange("b n e k -> (b n e) k")
+    scale_rows = W3_w_scales.rearrange("g q n -> q g n")
+    out_rows = out.rearrange("b n h -> (b n) h")
+
+    with ExitStack() as ctx:
+        const = ctx.enter_context(tc.tile_pool(name="const", bufs=1))
+        raw_pool = ctx.enter_context(tc.tile_pool(name="raw", bufs=ROW_TILES * AHEAD))
+        ordered_pool = ctx.enter_context(tc.tile_pool(name="ordered", bufs=ROW_TILES * 2))
+        grouped_pool = ctx.enter_context(tc.tile_pool(name="grouped", bufs=ROW_TILES * 2))
+        operand_pool = ctx.enter_context(tc.tile_pool(name="operand", bufs=ROW_TILES * 3))
+        words_pool = ctx.enter_context(tc.tile_pool(name="words", bufs=K_STEPS))
+        planes_pool = ctx.enter_context(tc.tile_pool(name="planes", bufs=ROUNDS))
+        message_pool = ctx.enter_context(tc.tile_pool(name="message", bufs=ROW_TILES * N_TILES))
+        acc_pool = ctx.enter_context(tc.psum_pool(name="acc", bufs=ROW_TILES * N_TILES))
+        bank_pool = ctx.enter_context(tc.psum_pool(name="bank", bufs=PSUM_BANKS - ROW_TILES * N_TILES))
+        ctx.enter_context(tc.manual_schedule())
+
+        ident = const.tile([P, P], F32)
+        make_identity(nc, ident[:])
+
+        mask_nodes = const.tile([NODES, EDGES], BF16)
+        nc.scalar.dma_start(out=mask_nodes[:], in_=mask_attend.rearrange("b n e -> (b n) e"))
+        bias_nodes = const.tile([NODES, H], BF16)
+        nc.scalar.dma_start(out=bias_nodes[:], in_=W3_b.partition_broadcast(NODES))
+        state_nodes = const.tile([NODES, H], BF16)
+        nc.scalar.dma_start(out=state_nodes[:], in_=h_V.rearrange("b n h -> (b n) h"))
+
+        raw_rounds = []
+        w_words = []
+        w_planes = []
+
+        def load_h2(r):
+            k_cols = slice(r * ROUND * K_PASS, (r + 1) * ROUND * K_PASS)
+            tiles = []
+            for t in range(ROW_TILES):
+                raw = raw_pool.tile([P, ROUND * K_PASS], BF16)
+                nc.sync.dma_start(out=raw[:], in_=h2_rows[t * P : (t + 1) * P, k_cols])
+                tiles.append(raw)
+            raw_rounds.append(tiles)
+
+        def load_weights(r):
+            planes = planes_pool.tile([P, ROUND, H], U8, align_bytes=64)
+            nc.vector.memset(planes[:].bitcast(I32), 0)
+            for first in range(SCALE_ROWS // 2):
+                partition = 32 * (first // 4) + first % 4
+                nc.sync.dma_start(
+                    out=planes[partition : P : P // 2].bitcast(I32),
+                    in_=scale_rows[first : SCALE_ROWS : SCALE_ROWS // 2, r * ROUND : (r + 1) * ROUND, :].bitcast(I32),
+                )
+            w_planes.append(planes)
+            for g in range(r * ROUND, (r + 1) * ROUND):
+                words = words_pool.tile([P, PAIR * H], U8, align_bytes=64)
+                nc.sync.dma_start(out=words[:].bitcast(I32), in_=W3_w_words[g].bitcast(I32))
+                w_words.append(words)
+
+        def load_step(s):
+            if s < ROUNDS:
+                load_h2(s)
+            if s >= 1:
+                load_weights(s - 1)
+
+        def sort_round(raw_tiles):
+            tiles = []
+            for t in range(ROW_TILES):
+                ordered = ordered_pool.tile([P, ROUND, PAIR, P], F32)
+                nc.vector.tensor_copy(
+                    out=ordered[:],
+                    in_=raw_tiles[t][:].bitcast(F32).rearrange("r (g p u) -> r g u p", p=P, u=PAIR),
+                )
+                tiles.append(ordered)
+            return tiles
+
+        def transpose_round(ordered_tiles):
+            tiles = []
+            for t in range(ROW_TILES):
+                grouped = grouped_pool.tile([P, ROUND * P * PACK], BF16, align_bytes=64)
+                grouped_words = grouped[:].bitcast(F32).rearrange("p (g r u) -> p g r u", r=P, u=PAIR)
+                for first in range(0, ROUND, BANK_STEPS):
+                    bank = bank_pool.tile([P, BANK_STEPS, PAIR, P], F32, tag="bank")
+                    for j in range(BANK_STEPS):
+                        for u in range(PAIR):
+                            nc.tensor.transpose(bank[:, j, u, :], ordered_tiles[t][:, first + j, u, :], ident[:])
+                    nc.scalar.copy(
+                        out=grouped_words[:, first : first + BANK_STEPS],
+                        in_=bank[:].rearrange("p g u r -> p g r u"),
+                    )
+                tiles.append(grouped)
+            return tiles
+
+        def quantise_round(grouped_tiles):
+            operands = []
+            for t in range(ROW_TILES):
+                codes = operand_pool.tile([P, ROUND * P], U32, align_bytes=64)
+                scales = operand_pool.tile([P, ROUND * P], U8, align_bytes=64)
+                nc.vector.quantize_mx(out=codes[:].bitcast(FP8X4), scales=scales[:], in_=grouped_tiles[t][:])
+                operands.append((codes, scales))
+            return operands
+
+        acc = []
+        for t in range(ROW_TILES):
+            banks = []
+            for h in range(N_TILES):
+                total = acc_pool.tile([P, N_TILE], F32)
+                banks.append(total)
+            acc.append(banks)
+
+        def multiply_round(r, operands):
+            for i in range(ROUND):
+                g = r * ROUND + i
+                rows = slice(i * P, (i + 1) * P)
+                for t in range(ROW_TILES):
+                    codes, scales = operands[t]
+                    for h in range(N_TILES):
+                        nc.tensor.matmul_mx(
+                            out=acc[t][h][:],
+                            lhsT=codes[:, rows].bitcast(FP8X4),
+                            lhsT_scale=scales[:, rows],
+                            rhs=w_words[g][:, h * PAIR * N_TILE : (h + 1) * PAIR * N_TILE].bitcast(FP4X4),
+                            rhs_scale=w_planes[r][:, i, h * N_TILE : (h + 1) * N_TILE],
+                            start=(g == 0),
+                            stop=(g == K_STEPS - 1),
+                        )
+
+        for s in range(AHEAD):
+            load_step(s)
+
+        ordered_tiles = sort_round(raw_rounds[0])
+        grouped_tiles = transpose_round(ordered_tiles)
+        ordered_tiles = sort_round(raw_rounds[1])
+        operands = quantise_round(grouped_tiles)
+
+        for r in range(ROUNDS - 1):
+            if r + AHEAD <= ROUNDS:
+                load_step(r + AHEAD)
+            grouped_tiles = transpose_round(ordered_tiles)
+            if r + 2 < ROUNDS:
+                ordered_tiles = sort_round(raw_rounds[r + 2])
+            next_operands = quantise_round(grouped_tiles)
+            multiply_round(r, operands)
+            operands = next_operands
+
+        select_T = const.tile([P, NODES * EDGES], F32)
+        nc.vector.memset(select_T[:], 0.0)
+        nc.vector.tensor_tensor(
+            out=select_T[0:NODES].rearrange("m (j e) -> m j e", e=EDGES),
+            in0=ident[0:NODES, 0:NODES].unsqueeze(2).to_broadcast([NODES, NODES, EDGES]),
+            in1=mask_nodes[:].unsqueeze(1).to_broadcast([NODES, NODES, EDGES]),
+            op=MULT,
+        )
+        select_bank = bank_pool.tile([P, ROW_TILES, P], F32, tag="bank")
+        for t in range(ROW_TILES):
+            nc.tensor.transpose(select_bank[:, t, :], select_T[:, t * P : (t + 1) * P], ident[:])
+        select = const.tile([P, ROW_TILES, P], F32)
+        nc.vector.tensor_copy(out=select[:], in_=select_bank[:])
+
+        share = const.tile([NODES, 1], F32)
+        nc.vector.tensor_reduce(out=share[:], in_=mask_nodes[:], axis=mybir.AxisListType.X, op=ADD)
+        nc.vector.tensor_scalar_mul(out=share[:], in0=share[:], scalar1=1.0 / DIVISOR)
+        base = const.tile([NODES, H], F32)
+        nc.vector.scalar_tensor_tensor(
+            out=base[:], in0=bias_nodes[:], scalar=share[:, 0:1], in1=state_nodes[:], op0=MULT, op1=ADD
+        )
+
+        multiply_round(ROUNDS - 1, operands)
+
+        messages = []
+        for t in range(ROW_TILES):
+            halves = []
+            for h in range(N_TILES):
+                message = message_pool.tile([P, N_TILE], F32)
+                if h == 0:
+                    nc.vector.tensor_copy(out=message[:], in_=acc[t][h][:])
+                else:
+                    nc.scalar.copy(out=message[:], in_=acc[t][h][:])
+                halves.append(message)
+            messages.append(halves)
+
+        summed = []
+        for h in range(N_TILES):
+            node_sum = bank_pool.tile([P, N_TILE], F32, tag="bank")
+            summed.append(node_sum)
+        for t in range(ROW_TILES):
+            for h in range(N_TILES):
+                nc.tensor.matmul(
+                    out=summed[h][:],
+                    lhsT=select[:, t, :],
+                    rhs=messages[t][h][:],
+                    start=(t == 0),
+                    stop=(t == ROW_TILES - 1),
+                )
+
+        result = const.tile([NODES, H], F32)
+        for h in range(N_TILES):
+            cols = slice(h * N_TILE, (h + 1) * N_TILE)
+            nc.vector.scalar_tensor_tensor(
+                out=result[:, cols], in0=summed[h][0:NODES, :], scalar=1.0 / DIVISOR, in1=base[:, cols], op0=MULT, op1=ADD
+            )
+            nc.sync.dma_start(out=out_rows[:, cols], in_=result[:, cols])

@@ -34,6 +34,7 @@ SCALE_ROWS = K_PASS // 32
 ROUND = 4
 ROUNDS = K_STEPS // ROUND
 BANK_STEPS = 2
+WORD_STEPS = 2
 AHEAD = 4
 
 FLOPS = 2 * NODES * EDGES * K * H
@@ -51,7 +52,7 @@ def tile_declayerj_pb_k_kernel(tc, h2, h_V, mask_attend, W3_w_words, W3_w_scales
         ordered_pool = ctx.enter_context(tc.tile_pool(name="ordered", bufs=ROW_TILES * 2))
         grouped_pool = ctx.enter_context(tc.tile_pool(name="grouped", bufs=ROW_TILES * 2))
         operand_pool = ctx.enter_context(tc.tile_pool(name="operand", bufs=ROW_TILES * 3))
-        words_pool = ctx.enter_context(tc.tile_pool(name="words", bufs=K_STEPS))
+        words_pool = ctx.enter_context(tc.tile_pool(name="words", bufs=K_STEPS // WORD_STEPS))
         planes_pool = ctx.enter_context(tc.tile_pool(name="planes", bufs=ROUNDS))
         message_pool = ctx.enter_context(tc.tile_pool(name="message", bufs=ROW_TILES * N_TILES))
         acc_pool = ctx.enter_context(tc.psum_pool(name="acc", bufs=ROW_TILES * N_TILES))
@@ -81,26 +82,31 @@ def tile_declayerj_pb_k_kernel(tc, h2, h_V, mask_attend, W3_w_words, W3_w_scales
                 tiles.append(raw)
             raw_rounds.append(tiles)
 
-        def load_weights(r):
+        def load_scales(r):
             planes = planes_pool.tile([P, ROUND, H], U8, align_bytes=64)
             nc.vector.memset(planes[:].bitcast(I32), 0)
-            for first in range(SCALE_ROWS // 2):
-                partition = 32 * (first // 4) + first % 4
+            for j in range(SCALE_ROWS // 4):
                 nc.sync.dma_start(
-                    out=planes[partition : P : P // 2].bitcast(I32),
-                    in_=scale_rows[first : SCALE_ROWS : SCALE_ROWS // 2, r * ROUND : (r + 1) * ROUND, :].bitcast(I32),
+                    out=planes[j : P : P // 4].bitcast(I32),
+                    in_=scale_rows[j : SCALE_ROWS : SCALE_ROWS // 4, r * ROUND : (r + 1) * ROUND, :].bitcast(I32),
                 )
             w_planes.append(planes)
-            for g in range(r * ROUND, (r + 1) * ROUND):
-                words = words_pool.tile([P, PAIR * H], U8, align_bytes=64)
-                nc.sync.dma_start(out=words[:].bitcast(I32), in_=W3_w_words[g].bitcast(I32))
+
+        def load_words(r):
+            for g in range(r * ROUND, (r + 1) * ROUND, WORD_STEPS):
+                words = words_pool.tile([P, WORD_STEPS, PAIR * H], U8, align_bytes=64)
+                nc.sync.dma_start(
+                    out=words[:].bitcast(I32),
+                    in_=W3_w_words[g : g + WORD_STEPS].rearrange("g p b -> p g b").bitcast(I32),
+                )
                 w_words.append(words)
 
         def load_step(s):
             if s < ROUNDS:
                 load_h2(s)
+                load_scales(s)
             if s >= 1:
-                load_weights(s - 1)
+                load_words(s - 1)
 
         def sort_round(raw_tiles):
             tiles = []
@@ -158,7 +164,7 @@ def tile_declayerj_pb_k_kernel(tc, h2, h_V, mask_attend, W3_w_words, W3_w_scales
                             out=acc[t][h][:],
                             lhsT=codes[:, rows].bitcast(FP8X4),
                             lhsT_scale=scales[:, rows],
-                            rhs=w_words[g][:, h * PAIR * N_TILE : (h + 1) * PAIR * N_TILE].bitcast(FP4X4),
+                            rhs=w_words[g // WORD_STEPS][:, g % WORD_STEPS, h * PAIR * N_TILE : (h + 1) * PAIR * N_TILE].bitcast(FP4X4),
                             rhs_scale=w_planes[r][:, i, h * N_TILE : (h + 1) * N_TILE],
                             start=(g == 0),
                             stop=(g == K_STEPS - 1),

@@ -49,7 +49,6 @@ def tile_declayerj_pb_k_kernel(tc, h2, h_V, mask_attend, W3_w_words, W3_w_scales
     with ExitStack() as ctx:
         const = ctx.enter_context(tc.tile_pool(name="const", bufs=1))
         raw_pool = ctx.enter_context(tc.tile_pool(name="raw", bufs=ROW_TILES * AHEAD))
-        ordered_pool = ctx.enter_context(tc.tile_pool(name="ordered", bufs=ROW_TILES * 2))
         grouped_pool = ctx.enter_context(tc.tile_pool(name="grouped", bufs=ROW_TILES * 2))
         operand_pool = ctx.enter_context(tc.tile_pool(name="operand", bufs=ROW_TILES * 3))
         words_pool = ctx.enter_context(tc.tile_pool(name="words", bufs=K_STEPS // WORD_STEPS))
@@ -108,27 +107,17 @@ def tile_declayerj_pb_k_kernel(tc, h2, h_V, mask_attend, W3_w_words, W3_w_scales
             if s >= 1:
                 load_words(s - 1)
 
-        def sort_round(raw_tiles):
+        def transpose_round(raw_tiles):
             tiles = []
             for t in range(ROW_TILES):
-                ordered = ordered_pool.tile([P, ROUND, PAIR, P], F32)
-                nc.vector.tensor_copy(
-                    out=ordered[:],
-                    in_=raw_tiles[t][:].bitcast(F32).rearrange("r (g p u) -> r g u p", p=P, u=PAIR),
-                )
-                tiles.append(ordered)
-            return tiles
-
-        def transpose_round(ordered_tiles):
-            tiles = []
-            for t in range(ROW_TILES):
+                raw_words = raw_tiles[t][:].bitcast(F32).rearrange("r (g p u) -> r g u p", p=P, u=PAIR)
                 grouped = grouped_pool.tile([P, ROUND * P * PACK], BF16, align_bytes=64)
                 grouped_words = grouped[:].bitcast(F32).rearrange("p (g r u) -> p g r u", r=P, u=PAIR)
                 for first in range(0, ROUND, BANK_STEPS):
                     bank = bank_pool.tile([P, BANK_STEPS, PAIR, P], F32, tag="bank")
                     for j in range(BANK_STEPS):
                         for u in range(PAIR):
-                            nc.tensor.transpose(bank[:, j, u, :], ordered_tiles[t][:, first + j, u, :], ident[:])
+                            nc.tensor.transpose(bank[:, j, u, :], raw_words[:, first + j, u, :], ident[:])
                     nc.scalar.copy(
                         out=grouped_words[:, first : first + BANK_STEPS],
                         in_=bank[:].rearrange("p g u r -> p g r u"),
@@ -173,18 +162,12 @@ def tile_declayerj_pb_k_kernel(tc, h2, h_V, mask_attend, W3_w_words, W3_w_scales
         for s in range(AHEAD):
             load_step(s)
 
-        ordered_tiles = sort_round(raw_rounds[0])
-        grouped_tiles = transpose_round(ordered_tiles)
-        ordered_tiles = sort_round(raw_rounds[1])
-        operands = quantise_round(grouped_tiles)
+        operands = quantise_round(transpose_round(raw_rounds[0]))
 
         for r in range(ROUNDS - 1):
             if r + AHEAD <= ROUNDS:
                 load_step(r + AHEAD)
-            grouped_tiles = transpose_round(ordered_tiles)
-            if r + 2 < ROUNDS:
-                ordered_tiles = sort_round(raw_rounds[r + 2])
-            next_operands = quantise_round(grouped_tiles)
+            next_operands = quantise_round(transpose_round(raw_rounds[r + 1]))
             multiply_round(r, operands)
             operands = next_operands
 

@@ -42,7 +42,7 @@ FLOPS = 2 * NODES * EDGES * K * H
 
 def tile_declayerj_pb_k_kernel(tc, h2, h_V, mask_attend, W3_w_words, W3_w_scales, W3_b, out):
     nc = tc.nc
-    h2_rows = h2.rearrange("b n e k -> (b n e) k")
+    h2_rows = h2.rearrange("b n e k -> (b n e) k").rearrange("(p t) k -> t p k", t=ROW_TILES)
     scale_rows = W3_w_scales.rearrange("g q n -> q g n")
     out_rows = out.rearrange("b n h -> (b n) h")
 
@@ -53,7 +53,7 @@ def tile_declayerj_pb_k_kernel(tc, h2, h_V, mask_attend, W3_w_words, W3_w_scales
         operand_pool = ctx.enter_context(tc.tile_pool(name="operand", bufs=ROW_TILES * 3))
         words_pool = ctx.enter_context(tc.tile_pool(name="words", bufs=K_STEPS // WORD_STEPS))
         planes_pool = ctx.enter_context(tc.tile_pool(name="planes", bufs=ROUNDS))
-        message_pool = ctx.enter_context(tc.tile_pool(name="message", bufs=ROW_TILES * N_TILES))
+        message_pool = ctx.enter_context(tc.tile_pool(name="message", bufs=N_TILES))
         acc_pool = ctx.enter_context(tc.psum_pool(name="acc", bufs=ROW_TILES * N_TILES))
         bank_pool = ctx.enter_context(tc.psum_pool(name="bank", bufs=PSUM_BANKS - ROW_TILES * N_TILES))
         ctx.enter_context(tc.manual_schedule())
@@ -61,6 +61,8 @@ def tile_declayerj_pb_k_kernel(tc, h2, h_V, mask_attend, W3_w_words, W3_w_scales
         ident = const.tile([P, P], F32)
         make_identity(nc, ident[:])
 
+        mask_rows = const.tile([P, ROW_TILES], BF16)
+        nc.scalar.dma_start(out=mask_rows[:], in_=mask_attend.rearrange("b n e -> (b n e)").rearrange("(p t) -> p t", t=ROW_TILES))
         mask_nodes = const.tile([NODES, EDGES], BF16)
         nc.scalar.dma_start(out=mask_nodes[:], in_=mask_attend.rearrange("b n e -> (b n) e"))
         bias_nodes = const.tile([NODES, H], BF16)
@@ -77,7 +79,7 @@ def tile_declayerj_pb_k_kernel(tc, h2, h_V, mask_attend, W3_w_words, W3_w_scales
             tiles = []
             for t in range(ROW_TILES):
                 raw = raw_pool.tile([P, ROUND * K_PASS], BF16)
-                nc.sync.dma_start(out=raw[:], in_=h2_rows[t * P : (t + 1) * P, k_cols])
+                nc.sync.dma_start(out=raw[:], in_=h2_rows[t, :, k_cols])
                 tiles.append(raw)
             raw_rounds.append(tiles)
 
@@ -104,8 +106,7 @@ def tile_declayerj_pb_k_kernel(tc, h2, h_V, mask_attend, W3_w_words, W3_w_scales
             if s < ROUNDS:
                 load_h2(s)
                 load_scales(s)
-            if s >= 1:
-                load_words(s - 1)
+                load_words(s)
 
         def transpose_round(raw_tiles):
             tiles = []
@@ -142,48 +143,46 @@ def tile_declayerj_pb_k_kernel(tc, h2, h_V, mask_attend, W3_w_words, W3_w_scales
                 banks.append(total)
             acc.append(banks)
 
-        def multiply_round(r, operands):
-            for i in range(ROUND):
+        def multiply(r, steps, banks, operands):
+            for i in steps:
                 g = r * ROUND + i
                 rows = slice(i * P, (i + 1) * P)
-                for t in range(ROW_TILES):
+                for t, h in banks:
                     codes, scales = operands[t]
-                    for h in range(N_TILES):
-                        nc.tensor.matmul_mx(
-                            out=acc[t][h][:],
-                            lhsT=codes[:, rows].bitcast(FP8X4),
-                            lhsT_scale=scales[:, rows],
-                            rhs=w_words[g // WORD_STEPS][:, g % WORD_STEPS, h * PAIR * N_TILE : (h + 1) * PAIR * N_TILE].bitcast(FP4X4),
-                            rhs_scale=w_planes[r][:, i, h * N_TILE : (h + 1) * N_TILE],
-                            start=(g == 0),
-                            stop=(g == K_STEPS - 1),
-                        )
+                    nc.tensor.matmul_mx(
+                        out=acc[t][h][:],
+                        lhsT=codes[:, rows].bitcast(FP8X4),
+                        lhsT_scale=scales[:, rows],
+                        rhs=w_words[g // WORD_STEPS][:, g % WORD_STEPS, h * PAIR * N_TILE : (h + 1) * PAIR * N_TILE].bitcast(FP4X4),
+                        rhs_scale=w_planes[r][:, i, h * N_TILE : (h + 1) * N_TILE],
+                        start=(g == 0),
+                        stop=(g == K_STEPS - 1),
+                    )
 
-        for s in range(AHEAD):
+        all_banks = [(t, h) for t in range(ROW_TILES) for h in range(N_TILES)]
+
+        for s in range(AHEAD - 1):
             load_step(s)
 
         operands = quantise_round(transpose_round(raw_rounds[0]))
 
         for r in range(ROUNDS - 1):
-            if r + AHEAD <= ROUNDS:
-                load_step(r + AHEAD)
+            if r + AHEAD - 1 < ROUNDS:
+                load_step(r + AHEAD - 1)
             next_operands = quantise_round(transpose_round(raw_rounds[r + 1]))
-            multiply_round(r, operands)
+            multiply(r, range(ROUND), all_banks, operands)
             operands = next_operands
 
-        select_T = const.tile([P, NODES * EDGES], F32)
-        nc.vector.memset(select_T[:], 0.0)
-        nc.vector.tensor_tensor(
-            out=select_T[0:NODES].rearrange("m (j e) -> m j e", e=EDGES),
-            in0=ident[0:NODES, 0:NODES].unsqueeze(2).to_broadcast([NODES, NODES, EDGES]),
-            in1=mask_nodes[:].unsqueeze(1).to_broadcast([NODES, NODES, EDGES]),
-            op=MULT,
+        select = const.tile([P, P], F32)
+        nc.vector.memset(select[:], 0.0)
+        nc.vector.tensor_reduce(
+            out=select[:, 0:NODES],
+            in_=ident[:].rearrange("p (m e) -> p m e", m=NODES),
+            axis=mybir.AxisListType.X,
+            op=ADD,
         )
-        select_bank = bank_pool.tile([P, ROW_TILES, P], F32, tag="bank")
-        for t in range(ROW_TILES):
-            nc.tensor.transpose(select_bank[:, t, :], select_T[:, t * P : (t + 1) * P], ident[:])
-        select = const.tile([P, ROW_TILES, P], F32)
-        nc.vector.tensor_copy(out=select[:], in_=select_bank[:])
+        mask_col = const.tile([P, ROW_TILES], F32)
+        nc.vector.tensor_copy(out=mask_col[:], in_=mask_rows[:])
 
         share = const.tile([NODES, 1], F32)
         nc.vector.tensor_reduce(out=share[:], in_=mask_nodes[:], axis=mybir.AxisListType.X, op=ADD)
@@ -193,33 +192,25 @@ def tile_declayerj_pb_k_kernel(tc, h2, h_V, mask_attend, W3_w_words, W3_w_scales
             out=base[:], in0=bias_nodes[:], scalar=share[:, 0:1], in1=state_nodes[:], op0=MULT, op1=ADD
         )
 
-        multiply_round(ROUNDS - 1, operands)
-
-        messages = []
-        for t in range(ROW_TILES):
-            halves = []
-            for h in range(N_TILES):
-                message = message_pool.tile([P, N_TILE], F32)
-                if h == 0:
-                    nc.vector.tensor_copy(out=message[:], in_=acc[t][h][:])
-                else:
-                    nc.scalar.copy(out=message[:], in_=acc[t][h][:])
-                halves.append(message)
-            messages.append(halves)
+        masked = []
+        for h in range(N_TILES):
+            for t in range(ROW_TILES):
+                multiply(ROUNDS - 1, range(ROUND), [(t, h)], operands)
+            first = message_pool.tile([P, N_TILE], F32)
+            nc.scalar.activation(
+                out=first[:], in_=acc[0][h][:], func=mybir.ActivationFunctionType.Copy, scale=mask_col[:, 0:1]
+            )
+            both = message_pool.tile([P, N_TILE], F32)
+            nc.vector.scalar_tensor_tensor(
+                out=both[:], in0=acc[1][h][:], scalar=mask_col[:, 1:2], in1=first[:], op0=MULT, op1=ADD
+            )
+            masked.append(both)
 
         summed = []
         for h in range(N_TILES):
             node_sum = bank_pool.tile([P, N_TILE], F32, tag="bank")
+            nc.tensor.matmul(out=node_sum[:], lhsT=select[:], rhs=masked[h][:], start=True, stop=True)
             summed.append(node_sum)
-        for t in range(ROW_TILES):
-            for h in range(N_TILES):
-                nc.tensor.matmul(
-                    out=summed[h][:],
-                    lhsT=select[:, t, :],
-                    rhs=messages[t][h][:],
-                    start=(t == 0),
-                    stop=(t == ROW_TILES - 1),
-                )
 
         result = const.tile([NODES, H], F32)
         for h in range(N_TILES):

@@ -32,7 +32,9 @@ N_TILES = H // N_TILE
 SCALE_ROWS = K_PASS // 32
 
 ROUND = 4
-ROUNDS = K_STEPS // ROUND
+STEPS = [2, 2] + [ROUND] * ((K_STEPS - 4) // ROUND)
+ROUNDS = len(STEPS)
+FIRST = [sum(STEPS[:r]) for r in range(ROUNDS)]
 BANK_STEPS = 2
 WORD_STEPS = 2
 AHEAD = 4
@@ -49,6 +51,7 @@ def tile_declayerj_pb_k_kernel(tc, h2, h_V, mask_attend, W3_w_words, W3_w_scales
     with ExitStack() as ctx:
         const = ctx.enter_context(tc.tile_pool(name="const", bufs=1))
         raw_pool = ctx.enter_context(tc.tile_pool(name="raw", bufs=ROW_TILES * AHEAD))
+        sorted_pool = ctx.enter_context(tc.tile_pool(name="sorted", bufs=ROW_TILES * 2))
         grouped_pool = ctx.enter_context(tc.tile_pool(name="grouped", bufs=ROW_TILES * 2))
         operand_pool = ctx.enter_context(tc.tile_pool(name="operand", bufs=ROW_TILES * 3))
         words_pool = ctx.enter_context(tc.tile_pool(name="words", bufs=K_STEPS // WORD_STEPS))
@@ -75,26 +78,26 @@ def tile_declayerj_pb_k_kernel(tc, h2, h_V, mask_attend, W3_w_words, W3_w_scales
         w_planes = []
 
         def load_h2(r):
-            k_cols = slice(r * ROUND * K_PASS, (r + 1) * ROUND * K_PASS)
+            k_cols = slice(FIRST[r] * K_PASS, (FIRST[r] + STEPS[r]) * K_PASS)
             tiles = []
             for t in range(ROW_TILES):
-                raw = raw_pool.tile([P, ROUND * K_PASS], BF16)
+                raw = raw_pool.tile([P, STEPS[r] * K_PASS], BF16)
                 nc.sync.dma_start(out=raw[:], in_=h2_rows[t, :, k_cols])
                 tiles.append(raw)
             raw_rounds.append(tiles)
 
         def load_scales(r):
-            planes = planes_pool.tile([P, ROUND, H], U8, align_bytes=64)
+            planes = planes_pool.tile([P, STEPS[r], H], U8, align_bytes=64)
             nc.vector.memset(planes[:].bitcast(I32), 0)
             for j in range(SCALE_ROWS // 4):
                 nc.sync.dma_start(
                     out=planes[j : P : P // 4].bitcast(I32),
-                    in_=scale_rows[j : SCALE_ROWS : SCALE_ROWS // 4, r * ROUND : (r + 1) * ROUND, :].bitcast(I32),
+                    in_=scale_rows[j : SCALE_ROWS : SCALE_ROWS // 4, FIRST[r] : FIRST[r] + STEPS[r], :].bitcast(I32),
                 )
             w_planes.append(planes)
 
         def load_words(r):
-            for g in range(r * ROUND, (r + 1) * ROUND, WORD_STEPS):
+            for g in range(FIRST[r], FIRST[r] + STEPS[r], WORD_STEPS):
                 words = words_pool.tile([P, WORD_STEPS, PAIR * H], U8, align_bytes=64)
                 nc.sync.dma_start(
                     out=words[:].bitcast(I32),
@@ -102,23 +105,28 @@ def tile_declayerj_pb_k_kernel(tc, h2, h_V, mask_attend, W3_w_words, W3_w_scales
                 )
                 w_words.append(words)
 
-        def load_step(s):
-            if s < ROUNDS:
-                load_h2(s)
-                load_scales(s)
-                load_words(s)
-
-        def transpose_round(raw_tiles):
+        def sort_round(r):
             tiles = []
             for t in range(ROW_TILES):
-                raw_words = raw_tiles[t][:].bitcast(F32).rearrange("r (g p u) -> r g u p", p=P, u=PAIR)
-                grouped = grouped_pool.tile([P, ROUND * P * PACK], BF16, align_bytes=64)
+                in_order = sorted_pool.tile([P, STEPS[r] * PAIR * P], F32)
+                nc.vector.tensor_copy(
+                    out=in_order[:].rearrange("r (g u p) -> r g u p", u=PAIR, p=P),
+                    in_=raw_rounds[r][t][:].bitcast(F32).rearrange("r (g p u) -> r g u p", p=P, u=PAIR),
+                )
+                tiles.append(in_order)
+            return tiles
+
+        def transpose_round(r, sorted_tiles):
+            tiles = []
+            for t in range(ROW_TILES):
+                words = sorted_tiles[t][:].rearrange("r (g u p) -> r g u p", u=PAIR, p=P)
+                grouped = grouped_pool.tile([P, STEPS[r] * P * PACK], BF16, align_bytes=64)
                 grouped_words = grouped[:].bitcast(F32).rearrange("p (g r u) -> p g r u", r=P, u=PAIR)
-                for first in range(0, ROUND, BANK_STEPS):
+                for first in range(0, STEPS[r], BANK_STEPS):
                     bank = bank_pool.tile([P, BANK_STEPS, PAIR, P], F32, tag="bank")
                     for j in range(BANK_STEPS):
                         for u in range(PAIR):
-                            nc.tensor.transpose(bank[:, j, u, :], raw_words[:, first + j, u, :], ident[:])
+                            nc.tensor.transpose(bank[:, j, u, :], words[:, first + j, u, :], ident[:])
                     nc.scalar.copy(
                         out=grouped_words[:, first : first + BANK_STEPS],
                         in_=bank[:].rearrange("p g u r -> p g r u"),
@@ -126,11 +134,11 @@ def tile_declayerj_pb_k_kernel(tc, h2, h_V, mask_attend, W3_w_words, W3_w_scales
                 tiles.append(grouped)
             return tiles
 
-        def quantise_round(grouped_tiles):
+        def quantise_round(r, grouped_tiles):
             operands = []
             for t in range(ROW_TILES):
-                codes = operand_pool.tile([P, ROUND * P], U32, align_bytes=64)
-                scales = operand_pool.tile([P, ROUND * P], U8, align_bytes=64)
+                codes = operand_pool.tile([P, STEPS[r] * P], U32, align_bytes=64)
+                scales = operand_pool.tile([P, STEPS[r] * P], U8, align_bytes=64)
                 nc.vector.quantize_mx(out=codes[:].bitcast(FP8X4), scales=scales[:], in_=grouped_tiles[t][:])
                 operands.append((codes, scales))
             return operands
@@ -143,9 +151,9 @@ def tile_declayerj_pb_k_kernel(tc, h2, h_V, mask_attend, W3_w_words, W3_w_scales
                 banks.append(total)
             acc.append(banks)
 
-        def multiply(r, steps, banks, operands):
-            for i in steps:
-                g = r * ROUND + i
+        def multiply(r, banks, operands):
+            for i in range(STEPS[r]):
+                g = FIRST[r] + i
                 rows = slice(i * P, (i + 1) * P)
                 for t, h in banks:
                     codes, scales = operands[t]
@@ -161,16 +169,25 @@ def tile_declayerj_pb_k_kernel(tc, h2, h_V, mask_attend, W3_w_words, W3_w_scales
 
         all_banks = [(t, h) for t in range(ROW_TILES) for h in range(N_TILES)]
 
-        for s in range(AHEAD - 1):
-            load_step(s)
+        def load_step(r):
+            if r < ROUNDS:
+                load_h2(r)
+                load_scales(r)
+            if 1 <= r <= ROUNDS:
+                load_words(r - 1)
 
-        operands = quantise_round(transpose_round(raw_rounds[0]))
+        for r in range(AHEAD):
+            load_step(r)
+
+        operands = quantise_round(0, transpose_round(0, sort_round(0)))
+        sorted_tiles = sort_round(1)
 
         for r in range(ROUNDS - 1):
-            if r + AHEAD - 1 < ROUNDS:
-                load_step(r + AHEAD - 1)
-            next_operands = quantise_round(transpose_round(raw_rounds[r + 1]))
-            multiply(r, range(ROUND), all_banks, operands)
+            load_step(r + AHEAD)
+            next_operands = quantise_round(r + 1, transpose_round(r + 1, sorted_tiles))
+            if r + 2 < ROUNDS:
+                sorted_tiles = sort_round(r + 2)
+            multiply(r, all_banks, operands)
             operands = next_operands
 
         select = const.tile([P, P], F32)
@@ -195,7 +212,7 @@ def tile_declayerj_pb_k_kernel(tc, h2, h_V, mask_attend, W3_w_words, W3_w_scales
         masked = []
         for h in range(N_TILES):
             for t in range(ROW_TILES):
-                multiply(ROUNDS - 1, range(ROUND), [(t, h)], operands)
+                multiply(ROUNDS - 1, [(t, h)], operands)
             first = message_pool.tile([P, N_TILE], F32)
             nc.scalar.activation(
                 out=first[:], in_=acc[0][h][:], func=mybir.ActivationFunctionType.Copy, scale=mask_col[:, 0:1]

@@ -184,8 +184,11 @@ def tile_declayerj_pb_k_kernel(tc, h2, h_V, mask_attend, W3_w_words, W3_w_scales
 
         for r in range(ROUNDS - 1):
             load_step(r + AHEAD)
-            next_operands = quantise_round(r + 1, transpose_round(r + 1, sorted_tiles))
-            if r + 2 < ROUNDS:
+            grouped_tiles = transpose_round(r + 1, sorted_tiles)
+            if 1 < r < ROUNDS - 2:
+                sorted_tiles = sort_round(r + 2)
+            next_operands = quantise_round(r + 1, grouped_tiles)
+            if r <= 1:
                 sorted_tiles = sort_round(r + 2)
             multiply(r, all_banks, operands)
             operands = next_operands

@@ -87,7 +87,7 @@ def tile_declayerj_pb_k_kernel(tc, h2, h_V, mask_attend, W3_w_words, W3_w_scales
             raw_rounds.append(tiles)
 
         def load_scales(r):
-            planes = planes_pool.tile([P, STEPS[r], H], U8, align_bytes=64)
+            planes = planes_pool.tile([P, STEPS[r], H], U8, align_bytes=256)
             nc.vector.memset(planes[:].bitcast(I32), 0)
             for j in range(SCALE_ROWS // 4):
                 nc.sync.dma_start(
@@ -98,7 +98,7 @@ def tile_declayerj_pb_k_kernel(tc, h2, h_V, mask_attend, W3_w_words, W3_w_scales
 
         def load_words(r):
             for g in range(FIRST[r], FIRST[r] + STEPS[r], WORD_STEPS):
-                words = words_pool.tile([P, WORD_STEPS, PAIR * H], U8, align_bytes=64)
+                words = words_pool.tile([P, WORD_STEPS, PAIR * H], U8, align_bytes=256)
                 nc.sync.dma_start(
                     out=words[:].bitcast(I32),
                     in_=W3_w_words[g : g + WORD_STEPS].rearrange("g p b -> p g b").bitcast(I32),
@@ -120,7 +120,7 @@ def tile_declayerj_pb_k_kernel(tc, h2, h_V, mask_attend, W3_w_words, W3_w_scales
             tiles = []
             for t in range(ROW_TILES):
                 words = sorted_tiles[t][:].rearrange("r (g u p) -> r g u p", u=PAIR, p=P)
-                grouped = grouped_pool.tile([P, STEPS[r] * P * PACK], BF16, align_bytes=64)
+                grouped = grouped_pool.tile([P, STEPS[r] * P * PACK], BF16, align_bytes=256)
                 grouped_words = grouped[:].bitcast(F32).rearrange("p (g r u) -> p g r u", r=P, u=PAIR)
                 for first in range(0, STEPS[r], BANK_STEPS):
                     bank = bank_pool.tile([P, BANK_STEPS, PAIR, P], F32, tag="bank")
@@ -137,8 +137,8 @@ def tile_declayerj_pb_k_kernel(tc, h2, h_V, mask_attend, W3_w_words, W3_w_scales
         def quantise_round(r, grouped_tiles):
             operands = []
             for t in range(ROW_TILES):
-                codes = operand_pool.tile([P, STEPS[r] * P], U32, align_bytes=64)
-                scales = operand_pool.tile([P, STEPS[r] * P], U8, align_bytes=64)
+                codes = operand_pool.tile([P, STEPS[r] * P], U32, align_bytes=256)
+                scales = operand_pool.tile([P, STEPS[r] * P], U8, align_bytes=256)
                 nc.vector.quantize_mx(out=codes[:].bitcast(FP8X4), scales=scales[:], in_=grouped_tiles[t][:])
                 operands.append((codes, scales))
             return operands

@@ -81,7 +81,7 @@ def tile_declayerj_pb_k_kernel(tc, h2, h_V, mask_attend, W3_w_words, W3_w_scales
             k_cols = slice(FIRST[r] * K_PASS, (FIRST[r] + STEPS[r]) * K_PASS)
             tiles = []
             for t in range(ROW_TILES):
-                raw = raw_pool.tile([P, STEPS[r] * K_PASS], BF16)
+                raw = raw_pool.tile([P, STEPS[r] * K_PASS], BF16, align_bytes=256)
                 nc.sync.dma_start(out=raw[:], in_=h2_rows[t, :, k_cols])
                 tiles.append(raw)
             raw_rounds.append(tiles)
@@ -108,7 +108,7 @@ def tile_declayerj_pb_k_kernel(tc, h2, h_V, mask_attend, W3_w_words, W3_w_scales
         def sort_round(r):
             tiles = []
             for t in range(ROW_TILES):
-                in_order = sorted_pool.tile([P, STEPS[r] * PAIR * P], F32)
+                in_order = sorted_pool.tile([P, STEPS[r] * PAIR * P], F32, align_bytes=256)
                 nc.vector.tensor_copy(
                     out=in_order[:].rearrange("r (g u p) -> r g u p", u=PAIR, p=P),
                     in_=raw_rounds[r][t][:].bitcast(F32).rearrange("r (g p u) -> r g u p", p=P, u=PAIR),

@@ -37,6 +37,7 @@ ROUNDS = len(STEPS)
 FIRST = [sum(STEPS[:r]) for r in range(ROUNDS)]
 BANK_STEPS = 2
 WORD_STEPS = 2
+SLOT = 256
 AHEAD = 4
 
 FLOPS = 2 * NODES * EDGES * K * H
@@ -65,13 +66,13 @@ def tile_declayerj_pb_k_kernel(tc, h2, h_V, mask_attend, W3_w_words, W3_w_scales
         make_identity(nc, ident[:])
 
         mask_rows = const.tile([P, ROW_TILES], BF16)
-        nc.scalar.dma_start(out=mask_rows[:], in_=mask_attend.rearrange("b n e -> (b n e)").rearrange("(p t) -> p t", t=ROW_TILES))
+        nc.gpsimd.dma_start(out=mask_rows[:], in_=mask_attend.rearrange("b n e -> (b n e)").rearrange("(p t) -> p t", t=ROW_TILES))
         mask_nodes = const.tile([NODES, EDGES], BF16)
-        nc.scalar.dma_start(out=mask_nodes[:], in_=mask_attend.rearrange("b n e -> (b n) e"))
+        nc.gpsimd.dma_start(out=mask_nodes[:], in_=mask_attend.rearrange("b n e -> (b n) e"))
         bias_nodes = const.tile([NODES, H], BF16)
-        nc.scalar.dma_start(out=bias_nodes[:], in_=W3_b.partition_broadcast(NODES))
+        nc.gpsimd.dma_start(out=bias_nodes[:], in_=W3_b.partition_broadcast(NODES))
         state_nodes = const.tile([NODES, H], BF16)
-        nc.scalar.dma_start(out=state_nodes[:], in_=h_V.rearrange("b n h -> (b n) h"))
+        nc.gpsimd.dma_start(out=state_nodes[:], in_=h_V.rearrange("b n h -> (b n) h"))
 
         raw_rounds = []
         w_words = []
@@ -137,9 +138,14 @@ def tile_declayerj_pb_k_kernel(tc, h2, h_V, mask_attend, W3_w_words, W3_w_scales
         def quantise_round(r, grouped_tiles):
             operands = []
             for t in range(ROW_TILES):
-                codes = operand_pool.tile([P, STEPS[r] * P], U32, align_bytes=256)
-                scales = operand_pool.tile([P, STEPS[r] * P], U8, align_bytes=256)
-                nc.vector.quantize_mx(out=codes[:].bitcast(FP8X4), scales=scales[:], in_=grouped_tiles[t][:])
+                codes = operand_pool.tile([P, STEPS[r], P], U32, align_bytes=256)
+                scales = operand_pool.tile([P, STEPS[r], SLOT], U8, align_bytes=256)
+                for i in range(STEPS[r]):
+                    nc.vector.quantize_mx(
+                        out=codes[:, i].bitcast(FP8X4),
+                        scales=scales[:, i, 0:P],
+                        in_=grouped_tiles[t][:, i * P * PACK : (i + 1) * P * PACK],
+                    )
                 operands.append((codes, scales))
             return operands
 
@@ -154,13 +160,12 @@ def tile_declayerj_pb_k_kernel(tc, h2, h_V, mask_attend, W3_w_words, W3_w_scales
         def multiply(r, banks, operands):
             for i in range(STEPS[r]):
                 g = FIRST[r] + i
-                rows = slice(i * P, (i + 1) * P)
                 for t, h in banks:
                     codes, scales = operands[t]
                     nc.tensor.matmul_mx(
                         out=acc[t][h][:],
-                        lhsT=codes[:, rows].bitcast(FP8X4),
-                        lhsT_scale=scales[:, rows],
+                        lhsT=codes[:, i].bitcast(FP8X4),
+                        lhsT_scale=scales[:, i, 0:P],
                         rhs=w_words[g // WORD_STEPS][:, g % WORD_STEPS, h * PAIR * N_TILE : (h + 1) * PAIR * N_TILE].bitcast(FP4X4),
                         rhs_scale=w_planes[r][:, i, h * N_TILE : (h + 1) * N_TILE],
                         start=(g == 0),
@@ -172,14 +177,17 @@ def tile_declayerj_pb_k_kernel(tc, h2, h_V, mask_attend, W3_w_words, W3_w_scales
         def load_step(r):
             if r < ROUNDS:
                 load_h2(r)
-                load_scales(r)
             if 1 <= r <= ROUNDS:
                 load_words(r - 1)
+            if r < ROUNDS:
+                load_scales(r)
 
-        for r in range(AHEAD):
+        for r in range(2):
             load_step(r)
-
-        operands = quantise_round(0, transpose_round(0, sort_round(0)))
+        grouped_tiles = transpose_round(0, sort_round(0))
+        for r in range(2, AHEAD):
+            load_step(r)
+        operands = quantise_round(0, grouped_tiles)
         sorted_tiles = sort_round(1)
 
         for r in range(ROUNDS - 1):
@@ -212,6 +220,7 @@ def tile_declayerj_pb_k_kernel(tc, h2, h_V, mask_attend, W3_w_words, W3_w_scales
             out=base[:], in0=bias_nodes[:], scalar=share[:, 0:1], in1=state_nodes[:], op0=MULT, op1=ADD
         )
 
+        parts = [(0, 0, N_TILE), (1, 0, N_TILE // 2), (1, N_TILE // 2, N_TILE)]
         masked = []
         for h in range(N_TILES):
             for t in range(ROW_TILES):
@@ -221,21 +230,33 @@ def tile_declayerj_pb_k_kernel(tc, h2, h_V, mask_attend, W3_w_words, W3_w_scales
                 out=first[:], in_=acc[0][h][:], func=mybir.ActivationFunctionType.Copy, scale=mask_col[:, 0:1]
             )
             both = message_pool.tile([P, N_TILE], F32)
-            nc.vector.scalar_tensor_tensor(
-                out=both[:], in0=acc[1][h][:], scalar=mask_col[:, 1:2], in1=first[:], op0=MULT, op1=ADD
-            )
+            for part_h, start, end in parts:
+                if part_h == h:
+                    nc.vector.scalar_tensor_tensor(
+                        out=both[:, start:end],
+                        in0=acc[1][h][:, start:end],
+                        scalar=mask_col[:, 1:2],
+                        in1=first[:, start:end],
+                        op0=MULT,
+                        op1=ADD,
+                    )
             masked.append(both)
 
         summed = []
-        for h in range(N_TILES):
+        for h, start, end in parts:
             node_sum = bank_pool.tile([P, N_TILE], F32, tag="bank")
-            nc.tensor.matmul(out=node_sum[:], lhsT=select[:], rhs=masked[h][:], start=True, stop=True)
+            nc.tensor.matmul(out=node_sum[:, 0 : end - start], lhsT=select[:], rhs=masked[h][:, start:end], start=True, stop=True)
             summed.append(node_sum)
 
         result = const.tile([NODES, H], F32)
-        for h in range(N_TILES):
-            cols = slice(h * N_TILE, (h + 1) * N_TILE)
+        for (h, start, end), node_sum, queue in zip(parts, summed, (nc.sync, nc.scalar, nc.sync)):
+            cols = slice(h * N_TILE + start, h * N_TILE + end)
             nc.vector.scalar_tensor_tensor(
-                out=result[:, cols], in0=summed[h][0:NODES, :], scalar=1.0 / DIVISOR, in1=base[:, cols], op0=MULT, op1=ADD
+                out=result[:, cols],
+                in0=node_sum[0:NODES, 0 : end - start],
+                scalar=1.0 / DIVISOR,
+                in1=base[:, cols],
+                op0=MULT,
+                op1=ADD,
             )
-            nc.sync.dma_start(out=out_rows[:, cols], in_=result[:, cols])
+            queue.dma_start(out=out_rows[:, cols], in_=result[:, cols])

@@ -74,6 +74,14 @@ def tile_declayerj_pb_k_kernel(tc, h2, h_V, mask_attend, W3_w_words, W3_w_scales
         state_nodes = const.tile([NODES, H], BF16)
         nc.gpsimd.dma_start(out=state_nodes[:], in_=h_V.rearrange("b n h -> (b n) h"))
 
+        idle = const.tile([P, N_TILE], BF16)
+        nc.vector.memset(idle[:].bitcast(I32), 0)
+
+        def warm_up(count):
+            for turn in range(count):
+                unread = bank_pool.tile([P, N_TILE], F32, tag="bank")
+                nc.tensor.matmul(out=unread[:], lhsT=idle[:, 0:P], rhs=idle[:], start=True, stop=True)
+
         raw_rounds = []
         w_words = []
         w_planes = []
@@ -87,15 +95,18 @@ def tile_declayerj_pb_k_kernel(tc, h2, h_V, mask_attend, W3_w_words, W3_w_scales
                 tiles.append(raw)
             raw_rounds.append(tiles)
 
-        def load_scales(r):
+        def zero_planes(r):
             planes = planes_pool.tile([P, STEPS[r], H], U8, align_bytes=256)
             nc.vector.memset(planes[:].bitcast(I32), 0)
+            w_planes.append(planes)
+
+        def load_scales(r):
+            planes = w_planes[r]
             for j in range(SCALE_ROWS // 4):
                 nc.sync.dma_start(
                     out=planes[j : P : P // 4].bitcast(I32),
                     in_=scale_rows[j : SCALE_ROWS : SCALE_ROWS // 4, FIRST[r] : FIRST[r] + STEPS[r], :].bitcast(I32),
                 )
-            w_planes.append(planes)
 
         def load_words(r):
             for g in range(FIRST[r], FIRST[r] + STEPS[r], WORD_STEPS):
@@ -140,13 +151,14 @@ def tile_declayerj_pb_k_kernel(tc, h2, h_V, mask_attend, W3_w_words, W3_w_scales
             for t in range(ROW_TILES):
                 codes = operand_pool.tile([P, STEPS[r], P], U32, align_bytes=256)
                 scales = operand_pool.tile([P, STEPS[r], SLOT], U8, align_bytes=256)
-                for i in range(STEPS[r]):
+                operands.append((codes, scales))
+            for i in range(STEPS[r]):
+                for t, (codes, scales) in enumerate(operands):
                     nc.vector.quantize_mx(
                         out=codes[:, i].bitcast(FP8X4),
                         scales=scales[:, i, 0:P],
                         in_=grouped_tiles[t][:, i * P * PACK : (i + 1) * P * PACK],
                     )
-                operands.append((codes, scales))
             return operands
 
         acc = []
@@ -178,26 +190,28 @@ def tile_declayerj_pb_k_kernel(tc, h2, h_V, mask_attend, W3_w_words, W3_w_scales
             if r < ROUNDS:
                 load_h2(r)
             if 1 <= r <= ROUNDS:
+                load_scales(r - 1)
                 load_words(r - 1)
-            if r < ROUNDS:
-                load_scales(r)
 
-        for r in range(2):
+        for r in range(3):
+            zero_planes(r)
             load_step(r)
+        warm_up(5)
         grouped_tiles = transpose_round(0, sort_round(0))
-        for r in range(2, AHEAD):
-            load_step(r)
-        operands = quantise_round(0, grouped_tiles)
+        warm_up(3)
         sorted_tiles = sort_round(1)
+        operands = quantise_round(0, grouped_tiles)
+        zero_planes(3)
+        load_step(3)
 
         for r in range(ROUNDS - 1):
-            load_step(r + AHEAD)
             grouped_tiles = transpose_round(r + 1, sorted_tiles)
-            if 1 < r < ROUNDS - 2:
+            if r < ROUNDS - 2:
                 sorted_tiles = sort_round(r + 2)
             next_operands = quantise_round(r + 1, grouped_tiles)
-            if r <= 1:
-                sorted_tiles = sort_round(r + 2)
+            if r + AHEAD < ROUNDS:
+                zero_planes(r + AHEAD)
+            load_step(r + AHEAD)
             multiply(r, all_banks, operands)
             operands = next_operands
 

from contextlib import ExitStack

import concourse.mybir as mybir
from concourse.masks import make_identity

F32 = mybir.dt.float32
BF16 = mybir.dt.bfloat16
I32 = mybir.dt.int32
U32 = mybir.dt.uint32
U8 = mybir.dt.uint8
FP8X4 = mybir.dt.float8_e4m3fn_x4
FP4X4 = mybir.dt.float4_e2m1fn_x4
ADD = mybir.AluOpType.add
MULT = mybir.AluOpType.mult

P = 128
PACK = 4
K_PASS = P * PACK
PAIR = 2

NODES = 16
EDGES = 16
K = 16384
H = 1024
DIVISOR = 30.0

ROW_TILES = NODES * EDGES // P
K_STEPS = K // K_PASS
PSUM_BANKS = 8
N_TILE = 512
N_TILES = H // N_TILE
SCALE_ROWS = K_PASS // 32

ROUND = 4
STEPS = [2, 2] + [ROUND] * ((K_STEPS - 4) // ROUND)
ROUNDS = len(STEPS)
FIRST = [sum(STEPS[:r]) for r in range(ROUNDS)]
BANK_STEPS = 2
WORD_STEPS = 2
SLOT = 256
AHEAD = 4

FLOPS = 2 * NODES * EDGES * K * H


def tile_declayerj_pb_k_kernel(tc, h2, h_V, mask_attend, W3_w_words, W3_w_scales, W3_b, out):
    nc = tc.nc
    h2_rows = h2.rearrange("b n e k -> (b n e) k").rearrange("(p t) k -> t p k", t=ROW_TILES)
    scale_rows = W3_w_scales.rearrange("g q n -> q g n")
    out_rows = out.rearrange("b n h -> (b n) h")

    with ExitStack() as ctx:
        const = ctx.enter_context(tc.tile_pool(name="const", bufs=1))
        raw_pool = ctx.enter_context(tc.tile_pool(name="raw", bufs=ROW_TILES * AHEAD))
        sorted_pool = ctx.enter_context(tc.tile_pool(name="sorted", bufs=ROW_TILES * 2))
        grouped_pool = ctx.enter_context(tc.tile_pool(name="grouped", bufs=ROW_TILES * 2))
        operand_pool = ctx.enter_context(tc.tile_pool(name="operand", bufs=ROW_TILES * 3))
        words_pool = ctx.enter_context(tc.tile_pool(name="words", bufs=K_STEPS // WORD_STEPS))
        planes_pool = ctx.enter_context(tc.tile_pool(name="planes", bufs=ROUNDS))
        message_pool = ctx.enter_context(tc.tile_pool(name="message", bufs=N_TILES))
        acc_pool = ctx.enter_context(tc.psum_pool(name="acc", bufs=ROW_TILES * N_TILES))
        bank_pool = ctx.enter_context(tc.psum_pool(name="bank", bufs=PSUM_BANKS - ROW_TILES * N_TILES))
        ctx.enter_context(tc.manual_schedule())

        ident = const.tile([P, P], F32)
        make_identity(nc, ident[:])

        mask_rows = const.tile([P, ROW_TILES], BF16)
        nc.gpsimd.dma_start(out=mask_rows[:], in_=mask_attend.rearrange("b n e -> (b n e)").rearrange("(p t) -> p t", t=ROW_TILES))
        mask_nodes = const.tile([NODES, EDGES], BF16)
        nc.gpsimd.dma_start(out=mask_nodes[:], in_=mask_attend.rearrange("b n e -> (b n) e"))
        bias_nodes = const.tile([NODES, H], BF16)
        nc.gpsimd.dma_start(out=bias_nodes[:], in_=W3_b.partition_broadcast(NODES))
        state_nodes = const.tile([NODES, H], BF16)
        nc.gpsimd.dma_start(out=state_nodes[:], in_=h_V.rearrange("b n h -> (b n) h"))

        idle = const.tile([P, N_TILE], BF16)
        nc.vector.memset(idle[:].bitcast(I32), 0)

        def warm_up(count):
            for turn in range(count):
                unread = bank_pool.tile([P, N_TILE], F32, tag="bank")
                nc.tensor.matmul(out=unread[:], lhsT=idle[:, 0:P], rhs=idle[:], start=True, stop=True)

        raw_rounds = []
        w_words = []
        w_planes = []

        def load_h2(r):
            k_cols = slice(FIRST[r] * K_PASS, (FIRST[r] + STEPS[r]) * K_PASS)
            tiles = []
            for t in range(ROW_TILES):
                raw = raw_pool.tile([P, STEPS[r] * K_PASS], BF16, align_bytes=256)
                nc.sync.dma_start(out=raw[:], in_=h2_rows[t, :, k_cols])
                tiles.append(raw)
            raw_rounds.append(tiles)

        def zero_planes(r):
            planes = planes_pool.tile([P, STEPS[r], H], U8, align_bytes=256)
            nc.vector.memset(planes[:].bitcast(I32), 0)
            w_planes.append(planes)

        def load_scales(r):
            planes = w_planes[r]
            for j in range(SCALE_ROWS // 4):
                nc.sync.dma_start(
                    out=planes[j : P : P // 4].bitcast(I32),
                    in_=scale_rows[j : SCALE_ROWS : SCALE_ROWS // 4, FIRST[r] : FIRST[r] + STEPS[r], :].bitcast(I32),
                )

        def load_words(r):
            for g in range(FIRST[r], FIRST[r] + STEPS[r], WORD_STEPS):
                words = words_pool.tile([P, WORD_STEPS, PAIR * H], U8, align_bytes=256)
                nc.sync.dma_start(
                    out=words[:].bitcast(I32),
                    in_=W3_w_words[g : g + WORD_STEPS].rearrange("g p b -> p g b").bitcast(I32),
                )
                w_words.append(words)

        def sort_round(r):
            tiles = []
            for t in range(ROW_TILES):
                in_order = sorted_pool.tile([P, STEPS[r] * PAIR * P], F32, align_bytes=256)
                nc.vector.tensor_copy(
                    out=in_order[:].rearrange("r (g u p) -> r g u p", u=PAIR, p=P),
                    in_=raw_rounds[r][t][:].bitcast(F32).rearrange("r (g p u) -> r g u p", p=P, u=PAIR),
                )
                tiles.append(in_order)
            return tiles

        def transpose_round(r, sorted_tiles):
            tiles = []
            for t in range(ROW_TILES):
                words = sorted_tiles[t][:].rearrange("r (g u p) -> r g u p", u=PAIR, p=P)
                grouped = grouped_pool.tile([P, STEPS[r] * P * PACK], BF16, align_bytes=256)
                grouped_words = grouped[:].bitcast(F32).rearrange("p (g r u) -> p g r u", r=P, u=PAIR)
                for first in range(0, STEPS[r], BANK_STEPS):
                    bank = bank_pool.tile([P, BANK_STEPS, PAIR, P], F32, tag="bank")
                    for j in range(BANK_STEPS):
                        for u in range(PAIR):
                            nc.tensor.transpose(bank[:, j, u, :], words[:, first + j, u, :], ident[:])
                    nc.scalar.copy(
                        out=grouped_words[:, first : first + BANK_STEPS],
                        in_=bank[:].rearrange("p g u r -> p g r u"),
                    )
                tiles.append(grouped)
            return tiles

        def quantise_round(r, grouped_tiles):
            operands = []
            for t in range(ROW_TILES):
                codes = operand_pool.tile([P, STEPS[r], P], U32, align_bytes=256)
                scales = operand_pool.tile([P, STEPS[r], SLOT], U8, align_bytes=256)
                operands.append((codes, scales))
            for i in range(STEPS[r]):
                for t, (codes, scales) in enumerate(operands):
                    nc.vector.quantize_mx(
                        out=codes[:, i].bitcast(FP8X4),
                        scales=scales[:, i, 0:P],
                        in_=grouped_tiles[t][:, i * P * PACK : (i + 1) * P * PACK],
                    )
            return operands

        acc = []
        for t in range(ROW_TILES):
            banks = []
            for h in range(N_TILES):
                total = acc_pool.tile([P, N_TILE], F32)
                banks.append(total)
            acc.append(banks)

        def multiply(r, banks, operands):
            for i in range(STEPS[r]):
                g = FIRST[r] + i
                for t, h in banks:
                    codes, scales = operands[t]
                    nc.tensor.matmul_mx(
                        out=acc[t][h][:],
                        lhsT=codes[:, i].bitcast(FP8X4),
                        lhsT_scale=scales[:, i, 0:P],
                        rhs=w_words[g // WORD_STEPS][:, g % WORD_STEPS, h * PAIR * N_TILE : (h + 1) * PAIR * N_TILE].bitcast(FP4X4),
                        rhs_scale=w_planes[r][:, i, h * N_TILE : (h + 1) * N_TILE],
                        start=(g == 0),
                        stop=(g == K_STEPS - 1),
                    )

        all_banks = [(t, h) for t in range(ROW_TILES) for h in range(N_TILES)]

        def load_step(r):
            if r < ROUNDS:
                load_h2(r)
            if 1 <= r <= ROUNDS:
                load_scales(r - 1)
                load_words(r - 1)

        for r in range(3):
            zero_planes(r)
            load_step(r)
        warm_up(5)
        grouped_tiles = transpose_round(0, sort_round(0))
        warm_up(3)
        sorted_tiles = sort_round(1)
        operands = quantise_round(0, grouped_tiles)
        zero_planes(3)
        load_step(3)

        for r in range(ROUNDS - 1):
            grouped_tiles = transpose_round(r + 1, sorted_tiles)
            if r < ROUNDS - 2:
                sorted_tiles = sort_round(r + 2)
            next_operands = quantise_round(r + 1, grouped_tiles)
            if r + AHEAD < ROUNDS:
                zero_planes(r + AHEAD)
            load_step(r + AHEAD)
            multiply(r, all_banks, operands)
            operands = next_operands

        select = const.tile([P, P], F32)
        nc.vector.memset(select[:], 0.0)
        nc.vector.tensor_reduce(
            out=select[:, 0:NODES],
            in_=ident[:].rearrange("p (m e) -> p m e", m=NODES),
            axis=mybir.AxisListType.X,
            op=ADD,
        )
        mask_col = const.tile([P, ROW_TILES], F32)
        nc.vector.tensor_copy(out=mask_col[:], in_=mask_rows[:])

        share = const.tile([NODES, 1], F32)
        nc.vector.tensor_reduce(out=share[:], in_=mask_nodes[:], axis=mybir.AxisListType.X, op=ADD)
        nc.vector.tensor_scalar_mul(out=share[:], in0=share[:], scalar1=1.0 / DIVISOR)
        base = const.tile([NODES, H], F32)
        nc.vector.scalar_tensor_tensor(
            out=base[:], in0=bias_nodes[:], scalar=share[:, 0:1], in1=state_nodes[:], op0=MULT, op1=ADD
        )

        parts = [(0, 0, N_TILE), (1, 0, N_TILE // 2), (1, N_TILE // 2, N_TILE)]
        masked = []
        for h in range(N_TILES):
            for t in range(ROW_TILES):
                multiply(ROUNDS - 1, [(t, h)], operands)
            first = message_pool.tile([P, N_TILE], F32)
            nc.scalar.activation(
                out=first[:], in_=acc[0][h][:], func=mybir.ActivationFunctionType.Copy, scale=mask_col[:, 0:1]
            )
            both = message_pool.tile([P, N_TILE], F32)
            for part_h, start, end in parts:
                if part_h == h:
                    nc.vector.scalar_tensor_tensor(
                        out=both[:, start:end],
                        in0=acc[1][h][:, start:end],
                        scalar=mask_col[:, 1:2],
                        in1=first[:, start:end],
                        op0=MULT,
                        op1=ADD,
                    )
            masked.append(both)

        summed = []
        for h, start, end in parts:
            node_sum = bank_pool.tile([P, N_TILE], F32, tag="bank")
            nc.tensor.matmul(out=node_sum[:, 0 : end - start], lhsT=select[:], rhs=masked[h][:, start:end], start=True, stop=True)
            summed.append(node_sum)

        result = const.tile([NODES, H], F32)
        for (h, start, end), node_sum, queue in zip(parts, summed, (nc.sync, nc.scalar, nc.sync)):
            cols = slice(h * N_TILE + start, h * N_TILE + end)
            nc.vector.scalar_tensor_tensor(
                out=result[:, cols],
                in0=node_sum[0:NODES, 0 : end - start],
                scalar=1.0 / DIVISOR,
                in1=base[:, cols],
                op0=MULT,
                op1=ADD,
            )
            queue.dma_start(out=out_rows[:, cols], in_=result[:, cols])
